import numpy as np
import ml_dtypes


def mxq(x, axis, fmt="e4m3"):
    dtype, down = {"e4m3": (ml_dtypes.float8_e4m3fn, 7), "e5m2": (ml_dtypes.float8_e5m2, 14)}[fmt]
    v = np.moveaxis(np.asarray(x, np.float32).astype(ml_dtypes.bfloat16).astype(np.float64), axis, -1)
    blocks = v.reshape(v.shape[:-1] + (-1, 32))
    amax = np.abs(blocks).max(-1, keepdims=True)
    byte = np.maximum(np.where(amax > 0, np.frexp(amax)[1] - 1 + 127, 0) - down, 1)
    scale = np.exp2(byte - 127.0)
    codes = (blocks / scale).astype(np.float32).astype(dtype).astype(np.float64)
    return np.moveaxis((codes * scale).reshape(v.shape), -1, axis)


WIDE = False


def mx_kscale(k):
    if not WIDE:
        return np.ones(k)
    levels = np.array([30, -30])
    if k % 512:
        return np.exp2(np.random.permutation(np.resize(levels, k // 32))).repeat(32)
    a = np.empty((k // 512, 16))
    for p in range(k // 512):
        a[p, :8] = np.random.permutation(np.resize(levels, 8))
        for g in range(8):
            far = levels[np.abs(levels - a[p, g]) >= 10]
            a[p, g + 8] = far[np.random.randint(len(far))]
    return np.exp2(a.ravel()).repeat(32)


BF16 = ml_dtypes.bfloat16


def bf(x):
    return np.asarray(x, np.float32).astype(BF16)


def f64(x):
    return np.asarray(x).astype(np.float64)


B, A, E, P, R = 256, 8, 512, 512, 512


def setup_inputs():
    s = mx_kscale(R)
    return {
        "attr_rep": bf(np.random.standard_normal((B, A, R)) * s),
        "bwd_proj": bf(np.random.standard_normal((A, R, P)) / np.sqrt(R) / s[:, None]),
        "self_weighted": bf(1.0 + 0.3 * np.random.standard_normal((1, A, 1))),
    }


def reference(attr_rep, bwd_proj, self_weighted):
    proj = (mxq(f64(attr_rep).transpose(1, 0, 2), 2, "e5m2") @ mxq(f64(bwd_proj), 1, "e5m2")).transpose(1, 0, 2)
    return np.sum(np.maximum(proj, 0.0) * f64(self_weighted), axis=1)

@@ -1,0 +1,166 @@
+from contextlib import ExitStack
+
+import concourse.mybir as mybir
+from concourse.masks import make_identity
+
+B, A, R, N = 256, 8, 512, 512
+FLOPS = 2 * B * A * R * N
+
+F32 = mybir.dt.float32
+BF16 = mybir.dt.bfloat16
+U32 = mybir.dt.uint32
+U8 = mybir.dt.uint8
+E5M2X4 = mybir.dt.float8_e5m2_x4
+ALU = mybir.AluOpType
+ACT = mybir.ActivationFunctionType
+
+P = 128
+PACK = 4
+B_TILES = B // P
+HALVES = 2
+RUN = 4
+VECTOR_COLUMNS_FIRST = 384
+VECTOR_COLUMNS = 144
+
+
+def tile_attributegnn_pb_kernel(tc, attr_rep, bwd_proj, self_weighted, out):
+    nc = tc.nc
+    last = A - 1
+
+    with ExitStack() as ctx:
+        keep = ctx.enter_context(tc.tile_pool(name="keep", bufs=1))
+        raw = ctx.enter_context(tc.tile_pool(name="raw", bufs=A))
+        work = ctx.enter_context(tc.tile_pool(name="work", bufs=3))
+        psum_sum = ctx.enter_context(tc.psum_pool(name="psum_sum", bufs=1))
+        psum_x = ctx.enter_context(tc.psum_pool(name="psum_x", bufs=2))
+        psum_proj = ctx.enter_context(tc.psum_pool(name="psum_proj", bufs=4))
+        ctx.enter_context(tc.manual_schedule())
+
+        x_raw, w_raw = [], []
+        for a in range(A):
+            x_tile = raw.tile([P, B_TILES, R], BF16, name="x_raw")
+            nc.sync.dma_start(out=x_tile[:], in_=attr_rep[:, a, :].rearrange("(t p) k -> p t k", p=P))
+            w_tile = raw.tile([P, PACK, N], BF16, name="w_raw")
+            nc.sync.dma_start(out=w_tile[:], in_=bwd_proj[a].rearrange("(p j) n -> p j n", j=PACK))
+            x_raw.append(x_tile)
+            w_raw.append(w_tile)
+
+        weight_bf16 = keep.tile([P, A], BF16)
+        nc.scalar.dma_start(
+            out=weight_bf16[:],
+            in_=self_weighted.rearrange("o a e -> (o a e)").partition_broadcast(P),
+        )
+        weight = keep.tile([P, A], F32)
+        nc.scalar.activation(out=weight[:], in_=weight_bf16[:], func=ACT.Copy)
+
+        identity = keep.tile([P, P], F32)
+        make_identity(nc, identity[:])
+
+        sums = [psum_sum.tile([P, N], F32, name="sum%d" % t) for t in range(B_TILES)]
+        x_turned, x_grouped, w_grouped, x_mx, w_mx, proj, terms = {}, {}, {}, {}, {}, {}, {}
+
+        def turn_x(a):
+            bank = psum_x.tile([P, B_TILES, 2, P], F32, name="x_turned")
+            for t in range(B_TILES):
+                words = x_raw[a][:, t, :].bitcast(F32)
+                for u in range(2):
+                    nc.tensor.transpose(bank[:, t, u, :], words[:, u : R // 2 : 2], identity[:])
+            x_turned[a] = bank
+
+        def group_x(a):
+            grouped = work.tile([P, B * PACK], BF16, name="x_grouped", align_bytes=64)
+            nc.scalar.copy(
+                out=grouped[:].bitcast(F32).rearrange("p (t r u) -> p t r u", t=B_TILES, u=2),
+                in_=x_turned[a][:].rearrange("p t u r -> p t r u"),
+            )
+            x_grouped[a] = grouped
+
+        def group_w(a, copy, columns):
+            if a not in w_grouped:
+                w_grouped[a] = work.tile([P, N, PACK], BF16, name="w_grouped", align_bytes=64)
+            copy(
+                out=w_grouped[a][:, columns, :].rearrange("p (c i) j -> p c j i", i=RUN),
+                in_=w_raw[a][:, :, columns].rearrange("p j (c i) -> p c j i", i=RUN),
+            )
+
+        def quantize(grouped, width, name):
+            codes = work.tile([P, width], U32, name=name + "_codes", align_bytes=64)
+            scales = work.tile([P, width], U8, name=name + "_scales", align_bytes=64)
+            nc.vector.quantize_mx(out=codes[:].bitcast(E5M2X4), scales=scales[:], in_=grouped)
+            return codes, scales
+
+        def multiply(target, stationary, columns, moving):
+            nc.tensor.matmul_mx(
+                out=target,
+                lhsT=stationary[0][:, columns].bitcast(E5M2X4),
+                lhsT_scale=stationary[1][:, columns],
+                rhs=moving[0][:].bitcast(E5M2X4),
+                rhs_scale=moving[1][:],
+                start=True,
+                stop=True,
+            )
+
+        def project_turned(a):
+            for h in range(HALVES):
+                bank = psum_proj.tile([P, N], F32, name="proj")
+                for c in range(2):
+                    n0 = (2 * h + c) * P
+                    multiply(bank[:, c * B : (c + 1) * B], w_mx[a], slice(n0, n0 + P), x_mx[a])
+                proj[a, h] = bank
+
+        def weigh(a, h):
+            term = work.tile([P, N], F32, name="term")
+            nc.vector.tensor_scalar(
+                out=term[:], in0=proj[a, h][:], scalar1=0.0, scalar2=weight[:, a : a + 1],
+                op0=ALU.max, op1=ALU.mult,
+            )
+            terms[a, h] = term
+
+        def add_turned(a, h):
+            for c in range(2):
+                n0 = (2 * h + c) * P
+                for t in range(B_TILES):
+                    b0 = c * B + t * P
+                    nc.tensor.matmul(
+                        out=sums[t][:, n0 : n0 + P],
+                        lhsT=terms[a, h][:, b0 : b0 + P],
+                        rhs=identity[:],
+                        is_transpose=True,
+                        start=(a == 0 and n0 == 0),
+                        stop=(a == last - 1 and n0 == N - P),
+                    )
+
+        def split(a):
+            return VECTOR_COLUMNS_FIRST if a == 0 else VECTOR_COLUMNS
+
+        turn_x(0)
+        group_x(0)
+        turn_x(1)
+        group_w(0, nc.vector.tensor_copy, slice(0, split(0)))
+        group_w(0, nc.scalar.copy, slice(split(0), N))
+        x_mx[0] = quantize(x_grouped[0][:], B, "x")
+        for a in range(last):
+            w_mx[a] = quantize(w_grouped[a][:].rearrange("p n j -> p (n j)"), N, "w")
+            group_x(a + 1)
+            project_turned(a)
+            if a + 2 < A:
+                turn_x(a + 2)
+            x_mx[a + 1] = quantize(x_grouped[a + 1][:], B, "x")
+            group_w(a + 1, nc.vector.tensor_copy, slice(0, split(a + 1)))
+            group_w(a + 1, nc.scalar.copy, slice(split(a + 1), N))
+            for h in range(HALVES):
+                weigh(a, h)
+                add_turned(a, h)
+
+        w_mx[last] = quantize(w_grouped[last][:].rearrange("p n j -> p (n j)"), N, "w")
+        for t in range(B_TILES):
+            bank = psum_proj.tile([P, N], F32, name="proj")
+            multiply(bank[:], x_mx[last], slice(t * P, (t + 1) * P), w_mx[last])
+            term = work.tile([P, N], F32, name="term")
+            nc.scalar.activation(out=term[:], in_=bank[:], func=ACT.Relu)
+            result = work.tile([P, N], F32, name="result")
+            nc.vector.scalar_tensor_tensor(
+                out=result[:], in0=term[:], scalar=weight[:, last : last + 1], in1=sums[t][:],
+                op0=ALU.mult, op1=ALU.add,
+            )
+            nc.sync.dma_start(out=out[t * P : (t + 1) * P, :], in_=result[:])

@@ -21,16 +21,17 @@ HALVES = 2
 RUN = 4
 VECTOR_COLUMNS_FIRST = 384
 VECTOR_COLUMNS = 144
+DIRECT = 2
 
 
 def tile_attributegnn_pb_kernel(tc, attr_rep, bwd_proj, self_weighted, out):
     nc = tc.nc
-    last = A - 1
+    turned = A - DIRECT
 
     with ExitStack() as ctx:
         keep = ctx.enter_context(tc.tile_pool(name="keep", bufs=1))
         raw = ctx.enter_context(tc.tile_pool(name="raw", bufs=A))
-        work = ctx.enter_context(tc.tile_pool(name="work", bufs=3))
+        work = ctx.enter_context(tc.tile_pool(name="work", bufs=4))
         psum_sum = ctx.enter_context(tc.psum_pool(name="psum_sum", bufs=1))
         psum_x = ctx.enter_context(tc.psum_pool(name="psum_x", bufs=2))
         psum_proj = ctx.enter_context(tc.psum_pool(name="psum_proj", bufs=4))
@@ -125,13 +126,29 @@ def tile_attributegnn_pb_kernel(tc, attr_rep, bwd_proj, self_weighted, out):
                         out=sums[t][:, n0 : n0 + P],
                         lhsT=terms[a, h][:, b0 : b0 + P],
                         rhs=identity[:],
-                        is_transpose=True,
+                        is_transpose=(n0 < N - P),
                         start=(a == 0 and n0 == 0),
-                        stop=(a == last - 1 and n0 == N - P),
+                        stop=(a == turned - 1 and n0 == N - P),
                     )
 
         def split(a):
-            return VECTOR_COLUMNS_FIRST if a == 0 else VECTOR_COLUMNS
+            return VECTOR_COLUMNS_FIRST if a < 2 else VECTOR_COLUMNS
+
+        def project_direct(a):
+            for t in range(B_TILES):
+                bank = psum_proj.tile([P, N], F32, name="proj")
+                multiply(bank[:], x_mx[a], slice(t * P, (t + 1) * P), w_mx[a])
+                proj[a, t] = bank
+
+        def add_direct(a, t, so_far):
+            term = work.tile([P, N], F32, name="term")
+            nc.scalar.activation(out=term[:], in_=proj[a, t][:], func=ACT.Relu)
+            result = work.tile([P, N], F32, name="result")
+            nc.vector.scalar_tensor_tensor(
+                out=result[:], in0=term[:], scalar=weight[:, a : a + 1], in1=so_far[:],
+                op0=ALU.mult, op1=ALU.add,
+            )
+            return result
 
         turn_x(0)
         group_x(0)
@@ -139,28 +156,28 @@ def tile_attributegnn_pb_kernel(tc, attr_rep, bwd_proj, self_weighted, out):
         group_w(0, nc.vector.tensor_copy, slice(0, split(0)))
         group_w(0, nc.scalar.copy, slice(split(0), N))
         x_mx[0] = quantize(x_grouped[0][:], B, "x")
-        for a in range(last):
+        for a in range(A):
             w_mx[a] = quantize(w_grouped[a][:].rearrange("p n j -> p (n j)"), N, "w")
-            group_x(a + 1)
-            project_turned(a)
+            if a < turned:
+                project_turned(a)
+            else:
+                project_direct(a)
             if a + 2 < A:
                 turn_x(a + 2)
-            x_mx[a + 1] = quantize(x_grouped[a + 1][:], B, "x")
-            group_w(a + 1, nc.vector.tensor_copy, slice(0, split(a + 1)))
-            group_w(a + 1, nc.scalar.copy, slice(split(a + 1), N))
-            for h in range(HALVES):
-                weigh(a, h)
-                add_turned(a, h)
+            if a + 1 < A:
+                group_x(a + 1)
+                group_w(a + 1, nc.vector.tensor_copy, slice(0, split(a + 1)))
+                group_w(a + 1, nc.scalar.copy, slice(split(a + 1), N))
+            if 0 <= a - 1 < turned:
+                for h in range(HALVES):
+                    weigh(a - 1, h)
+                    add_turned(a - 1, h)
+            if a + 1 < A:
+                x_mx[a + 1] = quantize(x_grouped[a + 1][:], B, "x")
 
-        w_mx[last] = quantize(w_grouped[last][:].rearrange("p n j -> p (n j)"), N, "w")
-        for t in range(B_TILES):
-            bank = psum_proj.tile([P, N], F32, name="proj")
-            multiply(bank[:], x_mx[last], slice(t * P, (t + 1) * P), w_mx[last])
-            term = work.tile([P, N], F32, name="term")
-            nc.scalar.activation(out=term[:], in_=bank[:], func=ACT.Relu)
-            result = work.tile([P, N], F32, name="result")
-            nc.vector.scalar_tensor_tensor(
-                out=result[:], in0=term[:], scalar=weight[:, last : last + 1], in1=sums[t][:],
-                op0=ALU.mult, op1=ALU.add,
-            )
-            nc.sync.dma_start(out=out[t * P : (t + 1) * P, :], in_=result[:])
+        totals = list(sums)
+        for a in range(turned, A):
+            for t in range(B_TILES):
+                totals[t] = add_direct(a, t, totals[t])
+                if a == A - 1:
+                    nc.sync.dma_start(out=out[t * P : (t + 1) * P, :], in_=totals[t][:])

@@ -19,8 +19,8 @@ PACK = 4
 B_TILES = B // P
 HALVES = 2
 RUN = 4
-VECTOR_COLUMNS_FIRST = 384
-VECTOR_COLUMNS = 144
+VECTOR_COLUMNS_FIRST = 352
+VECTOR_COLUMNS = 120
 DIRECT = 2
 
 
@@ -39,10 +39,10 @@ def tile_attributegnn_pb_kernel(tc, attr_rep, bwd_proj, self_weighted, out):
 
         x_raw, w_raw = [], []
         for a in range(A):
-            x_tile = raw.tile([P, B_TILES, R], BF16, name="x_raw")
-            nc.sync.dma_start(out=x_tile[:], in_=attr_rep[:, a, :].rearrange("(t p) k -> p t k", p=P))
             w_tile = raw.tile([P, PACK, N], BF16, name="w_raw")
             nc.sync.dma_start(out=w_tile[:], in_=bwd_proj[a].rearrange("(p j) n -> p j n", j=PACK))
+            x_tile = raw.tile([P, B_TILES, R], BF16, name="x_raw")
+            nc.sync.dma_start(out=x_tile[:], in_=attr_rep[:, a, :].rearrange("(t p) k -> p t k", p=P))
             x_raw.append(x_tile)
             w_raw.append(w_tile)
 
@@ -150,30 +150,35 @@ def tile_attributegnn_pb_kernel(tc, attr_rep, bwd_proj, self_weighted, out):
             )
             return result
 
+        def quantize_x(a):
+            x_mx[a] = quantize(x_grouped[a][:], B, "x")
+
+        last = A - 1
         turn_x(0)
-        group_x(0)
         turn_x(1)
         group_w(0, nc.vector.tensor_copy, slice(0, split(0)))
         group_w(0, nc.scalar.copy, slice(split(0), N))
-        x_mx[0] = quantize(x_grouped[0][:], B, "x")
         for a in range(A):
             w_mx[a] = quantize(w_grouped[a][:].rearrange("p n j -> p (n j)"), N, "w")
+            if a < last:
+                group_x(a)
+                if a + 1 == last:
+                    group_x(last)
+                group_w(a + 1, nc.vector.tensor_copy, slice(0, split(a + 1)))
+                group_w(a + 1, nc.scalar.copy, slice(split(a + 1), N))
+                quantize_x(a)
             if a < turned:
                 project_turned(a)
             else:
                 project_direct(a)
             if a + 2 < A:
                 turn_x(a + 2)
-            if a + 1 < A:
-                group_x(a + 1)
-                group_w(a + 1, nc.vector.tensor_copy, slice(0, split(a + 1)))
-                group_w(a + 1, nc.scalar.copy, slice(split(a + 1), N))
             if 0 <= a - 1 < turned:
                 for h in range(HALVES):
                     weigh(a - 1, h)
                     add_turned(a - 1, h)
-            if a + 1 < A:
-                x_mx[a + 1] = quantize(x_grouped[a + 1][:], B, "x")
+            if a + 1 == last:
+                quantize_x(last)
 
         totals = list(sums)
         for a in range(turned, A):

from contextlib import ExitStack

import concourse.mybir as mybir
from concourse.masks import make_identity

B, A, R, N = 256, 8, 512, 512
FLOPS = 2 * B * A * R * N

F32 = mybir.dt.float32
BF16 = mybir.dt.bfloat16
U32 = mybir.dt.uint32
U8 = mybir.dt.uint8
E5M2X4 = mybir.dt.float8_e5m2_x4
ALU = mybir.AluOpType
ACT = mybir.ActivationFunctionType

P = 128
PACK = 4
B_TILES = B // P
HALVES = 2
RUN = 4
VECTOR_COLUMNS_FIRST = 352
VECTOR_COLUMNS = 120
DIRECT = 2


def tile_attributegnn_pb_kernel(tc, attr_rep, bwd_proj, self_weighted, out):
    nc = tc.nc
    turned = A - DIRECT

    with ExitStack() as ctx:
        keep = ctx.enter_context(tc.tile_pool(name="keep", bufs=1))
        raw = ctx.enter_context(tc.tile_pool(name="raw", bufs=A))
        work = ctx.enter_context(tc.tile_pool(name="work", bufs=4))
        psum_sum = ctx.enter_context(tc.psum_pool(name="psum_sum", bufs=1))
        psum_x = ctx.enter_context(tc.psum_pool(name="psum_x", bufs=2))
        psum_proj = ctx.enter_context(tc.psum_pool(name="psum_proj", bufs=4))
        ctx.enter_context(tc.manual_schedule())

        x_raw, w_raw = [], []
        for a in range(A):
            w_tile = raw.tile([P, PACK, N], BF16, name="w_raw")
            nc.sync.dma_start(out=w_tile[:], in_=bwd_proj[a].rearrange("(p j) n -> p j n", j=PACK))
            x_tile = raw.tile([P, B_TILES, R], BF16, name="x_raw")
            nc.sync.dma_start(out=x_tile[:], in_=attr_rep[:, a, :].rearrange("(t p) k -> p t k", p=P))
            x_raw.append(x_tile)
            w_raw.append(w_tile)

        weight_bf16 = keep.tile([P, A], BF16)
        nc.scalar.dma_start(
            out=weight_bf16[:],
            in_=self_weighted.rearrange("o a e -> (o a e)").partition_broadcast(P),
        )
        weight = keep.tile([P, A], F32)
        nc.scalar.activation(out=weight[:], in_=weight_bf16[:], func=ACT.Copy)

        identity = keep.tile([P, P], F32)
        make_identity(nc, identity[:])

        sums = [psum_sum.tile([P, N], F32, name="sum%d" % t) for t in range(B_TILES)]
        x_turned, x_grouped, w_grouped, x_mx, w_mx, proj, terms = {}, {}, {}, {}, {}, {}, {}

        def turn_x(a):
            bank = psum_x.tile([P, B_TILES, 2, P], F32, name="x_turned")
            for t in range(B_TILES):
                words = x_raw[a][:, t, :].bitcast(F32)
                for u in range(2):
                    nc.tensor.transpose(bank[:, t, u, :], words[:, u : R // 2 : 2], identity[:])
            x_turned[a] = bank

        def group_x(a):
            grouped = work.tile([P, B * PACK], BF16, name="x_grouped", align_bytes=64)
            nc.scalar.copy(
                out=grouped[:].bitcast(F32).rearrange("p (t r u) -> p t r u", t=B_TILES, u=2),
                in_=x_turned[a][:].rearrange("p t u r -> p t r u"),
            )
            x_grouped[a] = grouped

        def group_w(a, copy, columns):
            if a not in w_grouped:
                w_grouped[a] = work.tile([P, N, PACK], BF16, name="w_grouped", align_bytes=64)
            copy(
                out=w_grouped[a][:, columns, :].rearrange("p (c i) j -> p c j i", i=RUN),
                in_=w_raw[a][:, :, columns].rearrange("p j (c i) -> p c j i", i=RUN),
            )

        def quantize(grouped, width, name):
            codes = work.tile([P, width], U32, name=name + "_codes", align_bytes=64)
            scales = work.tile([P, width], U8, name=name + "_scales", align_bytes=64)
            nc.vector.quantize_mx(out=codes[:].bitcast(E5M2X4), scales=scales[:], in_=grouped)
            return codes, scales

        def multiply(target, stationary, columns, moving):
            nc.tensor.matmul_mx(
                out=target,
                lhsT=stationary[0][:, columns].bitcast(E5M2X4),
                lhsT_scale=stationary[1][:, columns],
                rhs=moving[0][:].bitcast(E5M2X4),
                rhs_scale=moving[1][:],
                start=True,
                stop=True,
            )

        def project_turned(a):
            for h in range(HALVES):
                bank = psum_proj.tile([P, N], F32, name="proj")
                for c in range(2):
                    n0 = (2 * h + c) * P
                    multiply(bank[:, c * B : (c + 1) * B], w_mx[a], slice(n0, n0 + P), x_mx[a])
                proj[a, h] = bank

        def weigh(a, h):
            term = work.tile([P, N], F32, name="term")
            nc.vector.tensor_scalar(
                out=term[:], in0=proj[a, h][:], scalar1=0.0, scalar2=weight[:, a : a + 1],
                op0=ALU.max, op1=ALU.mult,
            )
            terms[a, h] = term

        def add_turned(a, h):
            for c in range(2):
                n0 = (2 * h + c) * P
                for t in range(B_TILES):
                    b0 = c * B + t * P
                    nc.tensor.matmul(
                        out=sums[t][:, n0 : n0 + P],
                        lhsT=terms[a, h][:, b0 : b0 + P],
                        rhs=identity[:],
                        is_transpose=(n0 < N - P),
                        start=(a == 0 and n0 == 0),
                        stop=(a == turned - 1 and n0 == N - P),
                    )

        def split(a):
            return VECTOR_COLUMNS_FIRST if a < 2 else VECTOR_COLUMNS

        def project_direct(a):
            for t in range(B_TILES):
                bank = psum_proj.tile([P, N], F32, name="proj")
                multiply(bank[:], x_mx[a], slice(t * P, (t + 1) * P), w_mx[a])
                proj[a, t] = bank

        def add_direct(a, t, so_far):
            term = work.tile([P, N], F32, name="term")
            nc.scalar.activation(out=term[:], in_=proj[a, t][:], func=ACT.Relu)
            result = work.tile([P, N], F32, name="result")
            nc.vector.scalar_tensor_tensor(
                out=result[:], in0=term[:], scalar=weight[:, a : a + 1], in1=so_far[:],
                op0=ALU.mult, op1=ALU.add,
            )
            return result

        def quantize_x(a):
            x_mx[a] = quantize(x_grouped[a][:], B, "x")

        last = A - 1
        turn_x(0)
        turn_x(1)
        group_w(0, nc.vector.tensor_copy, slice(0, split(0)))
        group_w(0, nc.scalar.copy, slice(split(0), N))
        for a in range(A):
            w_mx[a] = quantize(w_grouped[a][:].rearrange("p n j -> p (n j)"), N, "w")
            if a < last:
                group_x(a)
                if a + 1 == last:
                    group_x(last)
                group_w(a + 1, nc.vector.tensor_copy, slice(0, split(a + 1)))
                group_w(a + 1, nc.scalar.copy, slice(split(a + 1), N))
                quantize_x(a)
            if a < turned:
                project_turned(a)
            else:
                project_direct(a)
            if a + 2 < A:
                turn_x(a + 2)
            if 0 <= a - 1 < turned:
                for h in range(HALVES):
                    weigh(a - 1, h)
                    add_turned(a - 1, h)
            if a + 1 == last:
                quantize_x(last)

        totals = list(sums)
        for a in range(turned, A):
            for t in range(B_TILES):
                totals[t] = add_direct(a, t, totals[t])
                if a == A - 1:
                    nc.sync.dma_start(out=out[t * P : (t + 1) * P, :], in_=totals[t][:])
